import numpy as np
import ml_dtypes


def mxq(x, axis, fmt="e4m3"):
    dtype, down = {"e4m3": (ml_dtypes.float8_e4m3fn, 7), "e5m2": (ml_dtypes.float8_e5m2, 14)}[fmt]
    v = np.moveaxis(np.asarray(x, np.float32).astype(ml_dtypes.bfloat16).astype(np.float64), axis, -1)
    blocks = v.reshape(v.shape[:-1] + (-1, 32))
    amax = np.abs(blocks).max(-1, keepdims=True)
    byte = np.maximum(np.where(amax > 0, np.frexp(amax)[1] - 1 + 127, 0) - down, 1)
    scale = np.exp2(byte - 127.0)
    codes = (blocks / scale).astype(np.float32).astype(dtype).astype(np.float64)
    return np.moveaxis((codes * scale).reshape(v.shape), -1, axis)


WIDE = False


def mx_kscale(k):
    if not WIDE:
        return np.ones(k)
    levels = np.array([10, -10, 5, -5, 0])
    if k % 512:
        return np.exp2(np.random.permutation(np.resize(levels, k // 32))).repeat(32)
    a = np.empty((k // 512, 16))
    for p in range(k // 512):
        a[p, :8] = np.random.permutation(np.resize(levels, 8))
        for g in range(8):
            far = levels[np.abs(levels - a[p, g]) >= 10]
            a[p, g + 8] = far[np.random.randint(len(far))]
    return np.exp2(a.ravel()).repeat(32)


BF16 = ml_dtypes.bfloat16


def bf(x):
    return np.asarray(x, np.float32).astype(BF16)


def f64(x):
    return np.asarray(x).astype(np.float64)


B, C_IN, C_OUT, K, H, W = 2, 1024, 384, 3, 8, 8


def _shift2d(x, dh, dw):
    hh, ww = x.shape[2], x.shape[3]
    ph, pw = abs(dh), abs(dw)
    xp = np.pad(x, ((0, 0), (0, 0), (ph, ph), (pw, pw)))
    return xp[:, :, ph + dh: ph + dh + hh, pw + dw: pw + dw + ww]


def setup_inputs():
    s = mx_kscale(C_IN)
    bound = np.sqrt(2.0) * np.sqrt(3.0 / (C_IN * K))
    return {"x": bf(np.random.standard_normal((B, C_IN, H, W)) * s[None, :, None, None]),
            "weight": bf(np.random.uniform(-bound, bound, (C_OUT, C_IN, K)) / s[None, :, None]),
            "dilation": 1, "step": 1}


def reference(x, weight, dilation, step):
    nb, nc_in, nh, nw = x.shape
    no, nk = weight.shape[0], weight.shape[2]
    c0 = nk // 2
    xq = mxq(f64(x).reshape(nb, nc_in, nh * nw), 1, "e4m3")
    out = np.zeros((nb, no, nh, nw))
    for k in range(nk):
        off = k - c0
        y = mxq(f64(weight)[:, :, k], 1, "e4m3") @ xq
        out = out + _shift2d(y.reshape(nb, no, nh, nw), off * step, off * dilation)
    return out

@@ -1,0 +1,148 @@
+from contextlib import ExitStack
+
+import concourse.mybir as mybir
+from concourse.masks import make_identity
+
+BF16 = mybir.dt.bfloat16
+F32 = mybir.dt.float32
+I32 = mybir.dt.int32
+U32 = mybir.dt.uint32
+U8 = mybir.dt.uint8
+FP8X4 = mybir.dt.float8_e4m3fn_x4
+
+P = 128
+PACK = 4
+K_PASS = P * PACK
+
+B, C_IN, C_OUT, TAPS, H, W = 2, 1024, 384, 3, 8, 8
+PIXELS = B * H * W
+PASSES = C_IN // K_PASS
+O_TILES = C_OUT // P
+CHUNKS = O_TILES * PASSES
+X_ROUND = 2
+PSUM_BANKS = 8
+
+FLOPS = 2 * PIXELS * C_OUT * C_IN * TAPS
+
+
+def tile_skeletonconv_s_kernel(tc, x, weight, dilation, step, out):
+    nc = tc.nc
+    with ExitStack() as ctx:
+        keep = ctx.enter_context(tc.tile_pool(name="keep", bufs=1))
+        raw_pool = ctx.enter_context(tc.tile_pool(name="raw", bufs=CHUNKS))
+        grouped_pool = ctx.enter_context(tc.tile_pool(name="grouped", bufs=3 * TAPS))
+        result_pool = ctx.enter_context(tc.tile_pool(name="result", bufs=O_TILES))
+        flipped_pool = ctx.enter_context(tc.psum_pool(name="flipped", bufs=PSUM_BANKS - O_TILES))
+        acc_pool = ctx.enter_context(tc.psum_pool(name="acc", bufs=O_TILES))
+        ctx.enter_context(tc.manual_schedule())
+
+        x_raw = keep.tile([P, B, PASSES, PACK, H * W], BF16)
+        w_raw = []
+        for chunk in range(CHUNKS):
+            if chunk == X_ROUND:
+                nc.sync.dma_start(
+                    out=x_raw[:].rearrange("p b g v s -> p (b g) (v s)"),
+                    in_=x.rearrange("b (g p v) h w -> p (b g) (v h w)", g=PASSES, v=PACK, p=P),
+                )
+            ot, g = divmod(chunk, PASSES)
+            rows = raw_pool.tile([P, K_PASS * TAPS], BF16, name="rows")
+            nc.sync.dma_start(
+                out=rows[:],
+                in_=weight[ot * P : (ot + 1) * P, g * K_PASS : (g + 1) * K_PASS].rearrange("o c t -> o (c t)"),
+            )
+            w_raw.append(rows)
+
+        identity = keep.tile([P, P], BF16)
+        make_identity(nc, identity[:])
+
+        x_taps = keep.tile([P, TAPS, PASSES, B, H, W, PACK], BF16, align_bytes=64)
+        x_codes = keep.tile([P, TAPS, PASSES, PIXELS], U32, align_bytes=64)
+        x_scales = keep.tile([P, TAPS, PASSES, PIXELS], U8, align_bytes=64)
+        nc.vector.memset(x_taps[:].rearrange("p t g b h w v -> p (t g b h w v)").bitcast(I32), 0)
+        centre = TAPS // 2
+
+        def shift_x():
+            for g in range(PASSES):
+                nc.vector.tensor_copy(
+                    out=x_taps[:, centre, g].rearrange("p b h w v -> p b (h w) v"),
+                    in_=x_raw[:, :, g].rearrange("p b v s -> p b s v"),
+                )
+            for t in range(TAPS):
+                if t == centre:
+                    continue
+                dh, dw = (t - centre) * step, (t - centre) * dilation
+                h_lo, h_hi = max(0, -dh), H - max(0, dh)
+                w_lo, w_hi = max(0, -dw), W - max(0, dw)
+                nc.vector.tensor_copy(
+                    out=x_taps[:, t, :, :, h_lo:h_hi, w_lo:w_hi, :],
+                    in_=x_taps[:, centre, :, :, h_lo + dh : h_hi + dh, w_lo + dw : w_hi + dw, :],
+                )
+
+        def quantise_x():
+            for t in range(TAPS):
+                nc.vector.quantize_mx(
+                    out=x_codes[:, t].rearrange("p g n -> p (g n)").bitcast(FP8X4),
+                    scales=x_scales[:, t].rearrange("p g n -> p (g n)"),
+                    in_=x_taps[:, t].rearrange("p g b h w v -> p (g b h w v)"),
+                )
+
+        w_codes = keep.tile([P, CHUNKS, TAPS, P], U32, align_bytes=64)
+        w_scales = keep.tile([P, CHUNKS, TAPS, P], U8, align_bytes=64)
+        w_flipped, w_grouped, acc = {}, {}, {}
+
+        def flip(chunk):
+            by_value = w_raw[chunk][:].rearrange("o (c v t) -> o t v c", v=PACK, t=TAPS)
+            for t in range(TAPS):
+                flipped = flipped_pool.tile([P, PACK, P], BF16, name="flipped")
+                for v in range(PACK):
+                    nc.tensor.transpose(flipped[:, v, :], by_value[:, t, v], identity[:])
+                w_flipped[chunk, t] = flipped
+
+        def group(chunk):
+            for t in range(TAPS):
+                grouped = grouped_pool.tile([P, P, PACK], BF16, name="grouped", align_bytes=64)
+                nc.scalar.copy(out=grouped[:], in_=w_flipped[chunk, t][:].rearrange("p v o -> p o v"))
+                w_grouped[chunk, t] = grouped
+
+        def quantise(chunk):
+            for t in range(TAPS):
+                nc.vector.quantize_mx(
+                    out=w_codes[:, chunk, t].bitcast(FP8X4),
+                    scales=w_scales[:, chunk, t],
+                    in_=w_grouped[chunk, t][:].rearrange("p o v -> p (o v)"),
+                )
+
+        def multiply(chunk):
+            ot, g = divmod(chunk, PASSES)
+            if g == 0:
+                acc[ot] = acc_pool.tile([P, PIXELS], F32, name="acc")
+            for t in range(TAPS):
+                nc.tensor.matmul_mx(
+                    out=acc[ot][:],
+                    lhsT=w_codes[:, chunk, t].bitcast(FP8X4),
+                    lhsT_scale=w_scales[:, chunk, t],
+                    rhs=x_codes[:, t, g].bitcast(FP8X4),
+                    rhs_scale=x_scales[:, t, g],
+                    start=(g == 0 and t == 0),
+                    stop=(g == PASSES - 1 and t == TAPS - 1),
+                )
+            if g == PASSES - 1:
+                result = result_pool.tile([P, B, H * W], F32, name="result")
+                nc.scalar.copy(out=result[:].rearrange("p b s -> p (b s)"), in_=acc[ot][:])
+                nc.sync.dma_start(
+                    out=out[:, ot * P : (ot + 1) * P].rearrange("b o h w -> o b (h w)"), in_=result[:]
+                )
+
+        for rnd in range(CHUNKS + 2):
+            if rnd < CHUNKS:
+                flip(rnd)
+            if 0 <= rnd - 1 < CHUNKS:
+                group(rnd - 1)
+            if 0 <= rnd - 2 < CHUNKS:
+                quantise(rnd - 2)
+            if rnd == X_ROUND:
+                shift_x()
+            if rnd == X_ROUND + 1:
+                quantise_x()
+        for chunk in range(CHUNKS):
+            multiply(chunk)

@@ -19,8 +19,10 @@ PIXELS = B * H * W
 PASSES = C_IN // K_PASS
 O_TILES = C_OUT // P
 CHUNKS = O_TILES * PASSES
-X_ROUND = 2
-PSUM_BANKS = 8
+UNITS = CHUNKS * TAPS
+ACC_BANKS = 2
+FLIPPED_BANKS = 8 - ACC_BANKS
+VECTOR_EVERY = 5
 
 FLOPS = 2 * PIXELS * C_OUT * C_IN * TAPS
 
@@ -30,20 +32,19 @@ def tile_skeletonconv_s_kernel(tc, x, weight, dilation, step, out):
     with ExitStack() as ctx:
         keep = ctx.enter_context(tc.tile_pool(name="keep", bufs=1))
         raw_pool = ctx.enter_context(tc.tile_pool(name="raw", bufs=CHUNKS))
-        grouped_pool = ctx.enter_context(tc.tile_pool(name="grouped", bufs=3 * TAPS))
+        grouped_pool = ctx.enter_context(tc.tile_pool(name="grouped", bufs=6))
         result_pool = ctx.enter_context(tc.tile_pool(name="result", bufs=O_TILES))
-        flipped_pool = ctx.enter_context(tc.psum_pool(name="flipped", bufs=PSUM_BANKS - O_TILES))
-        acc_pool = ctx.enter_context(tc.psum_pool(name="acc", bufs=O_TILES))
+        flipped_pool = ctx.enter_context(tc.psum_pool(name="flipped", bufs=FLIPPED_BANKS))
+        acc_pool = ctx.enter_context(tc.psum_pool(name="acc", bufs=ACC_BANKS))
         ctx.enter_context(tc.manual_schedule())
 
         x_raw = keep.tile([P, B, PASSES, PACK, H * W], BF16)
+        nc.sync.dma_start(
+            out=x_raw[:].rearrange("p b g v s -> p (b g) (v s)"),
+            in_=x.rearrange("b (g p v) h w -> p (b g) (v h w)", g=PASSES, v=PACK, p=P),
+        )
         w_raw = []
         for chunk in range(CHUNKS):
-            if chunk == X_ROUND:
-                nc.sync.dma_start(
-                    out=x_raw[:].rearrange("p b g v s -> p (b g) (v s)"),
-                    in_=x.rearrange("b (g p v) h w -> p (b g) (v h w)", g=PASSES, v=PACK, p=P),
-                )
             ot, g = divmod(chunk, PASSES)
             rows = raw_pool.tile([P, K_PASS * TAPS], BF16, name="rows")
             nc.sync.dma_start(
@@ -58,91 +59,85 @@ def tile_skeletonconv_s_kernel(tc, x, weight, dilation, step, out):
         x_taps = keep.tile([P, TAPS, PASSES, B, H, W, PACK], BF16, align_bytes=64)
         x_codes = keep.tile([P, TAPS, PASSES, PIXELS], U32, align_bytes=64)
         x_scales = keep.tile([P, TAPS, PASSES, PIXELS], U8, align_bytes=64)
-        nc.vector.memset(x_taps[:].rearrange("p t g b h w v -> p (t g b h w v)").bitcast(I32), 0)
         centre = TAPS // 2
+        for t in range(TAPS):
+            if t != centre:
+                nc.vector.memset(x_taps[:, t].rearrange("p g b h w v -> p (g b h w v)").bitcast(I32), 0)
+        for g in range(PASSES):
+            nc.vector.tensor_copy(
+                out=x_taps[:, centre, g].rearrange("p b h w v -> p b (h w) v"),
+                in_=x_raw[:, :, g].rearrange("p b v s -> p b s v"),
+            )
+        for t in range(TAPS):
+            if t == centre:
+                continue
+            dh, dw = (t - centre) * step, (t - centre) * dilation
+            h_lo, h_hi = max(0, -dh), H - max(0, dh)
+            w_lo, w_hi = max(0, -dw), W - max(0, dw)
+            nc.vector.tensor_copy(
+                out=x_taps[:, t, :, :, h_lo:h_hi, w_lo:w_hi, :],
+                in_=x_taps[:, centre, :, :, h_lo + dh : h_hi + dh, w_lo + dw : w_hi + dw, :],
+            )
+        for t in (centre, *(t for t in range(TAPS) if t != centre)):
+            nc.vector.quantize_mx(
+                out=x_codes[:, t].rearrange("p g n -> p (g n)").bitcast(FP8X4),
+                scales=x_scales[:, t].rearrange("p g n -> p (g n)"),
+                in_=x_taps[:, t].rearrange("p g b h w v -> p (g b h w v)"),
+            )
 
-        def shift_x():
-            for g in range(PASSES):
-                nc.vector.tensor_copy(
-                    out=x_taps[:, centre, g].rearrange("p b h w v -> p b (h w) v"),
-                    in_=x_raw[:, :, g].rearrange("p b v s -> p b s v"),
-                )
-            for t in range(TAPS):
-                if t == centre:
-                    continue
-                dh, dw = (t - centre) * step, (t - centre) * dilation
-                h_lo, h_hi = max(0, -dh), H - max(0, dh)
-                w_lo, w_hi = max(0, -dw), W - max(0, dw)
-                nc.vector.tensor_copy(
-                    out=x_taps[:, t, :, :, h_lo:h_hi, w_lo:w_hi, :],
-                    in_=x_taps[:, centre, :, :, h_lo + dh : h_hi + dh, w_lo + dw : w_hi + dw, :],
-                )
-
-        def quantise_x():
-            for t in range(TAPS):
-                nc.vector.quantize_mx(
-                    out=x_codes[:, t].rearrange("p g n -> p (g n)").bitcast(FP8X4),
-                    scales=x_scales[:, t].rearrange("p g n -> p (g n)"),
-                    in_=x_taps[:, t].rearrange("p g b h w v -> p (g b h w v)"),
-                )
-
-        w_codes = keep.tile([P, CHUNKS, TAPS, P], U32, align_bytes=64)
-        w_scales = keep.tile([P, CHUNKS, TAPS, P], U8, align_bytes=64)
+        w_codes = keep.tile([P, UNITS, P], U32, align_bytes=64)
+        w_scales = keep.tile([P, UNITS, P], U8, align_bytes=64)
         w_flipped, w_grouped, acc = {}, {}, {}
 
-        def flip(chunk):
+        def flip(unit):
+            chunk, t = divmod(unit, TAPS)
             by_value = w_raw[chunk][:].rearrange("o (c v t) -> o t v c", v=PACK, t=TAPS)
-            for t in range(TAPS):
-                flipped = flipped_pool.tile([P, PACK, P], BF16, name="flipped")
-                for v in range(PACK):
-                    nc.tensor.transpose(flipped[:, v, :], by_value[:, t, v], identity[:])
-                w_flipped[chunk, t] = flipped
+            flipped = flipped_pool.tile([P, PACK, P], BF16, name="flipped")
+            for v in range(PACK):
+                nc.tensor.transpose(flipped[:, v, :], by_value[:, t, v], identity[:])
+            w_flipped[unit] = flipped
 
-        def group(chunk):
-            for t in range(TAPS):
-                grouped = grouped_pool.tile([P, P, PACK], BF16, name="grouped", align_bytes=64)
-                nc.scalar.copy(out=grouped[:], in_=w_flipped[chunk, t][:].rearrange("p v o -> p o v"))
-                w_grouped[chunk, t] = grouped
+        def group(unit):
+            grouped = grouped_pool.tile([P, P, PACK], BF16, name="grouped", align_bytes=64)
+            copy = nc.vector.tensor_copy if unit * 2 % VECTOR_EVERY >= VECTOR_EVERY - 2 else nc.scalar.copy
+            copy(out=grouped[:], in_=w_flipped[unit][:].rearrange("p v o -> p o v"))
+            w_grouped[unit] = grouped
 
-        def quantise(chunk):
-            for t in range(TAPS):
-                nc.vector.quantize_mx(
-                    out=w_codes[:, chunk, t].bitcast(FP8X4),
-                    scales=w_scales[:, chunk, t],
-                    in_=w_grouped[chunk, t][:].rearrange("p o v -> p (o v)"),
-                )
+        def quantise(unit):
+            nc.vector.quantize_mx(
+                out=w_codes[:, unit].bitcast(FP8X4),
+                scales=w_scales[:, unit],
+                in_=w_grouped[unit][:].rearrange("p o v -> p (o v)"),
+            )
 
-        def multiply(chunk):
+        def multiply(unit):
+            chunk, t = divmod(unit, TAPS)
             ot, g = divmod(chunk, PASSES)
-            if g == 0:
+            first, last = g == 0 and t == 0, g == PASSES - 1 and t == TAPS - 1
+            if first:
                 acc[ot] = acc_pool.tile([P, PIXELS], F32, name="acc")
-            for t in range(TAPS):
-                nc.tensor.matmul_mx(
-                    out=acc[ot][:],
-                    lhsT=w_codes[:, chunk, t].bitcast(FP8X4),
-                    lhsT_scale=w_scales[:, chunk, t],
-                    rhs=x_codes[:, t, g].bitcast(FP8X4),
-                    rhs_scale=x_scales[:, t, g],
-                    start=(g == 0 and t == 0),
-                    stop=(g == PASSES - 1 and t == TAPS - 1),
-                )
-            if g == PASSES - 1:
+            nc.tensor.matmul_mx(
+                out=acc[ot][:],
+                lhsT=w_codes[:, unit].bitcast(FP8X4),
+                lhsT_scale=w_scales[:, unit],
+                rhs=x_codes[:, t, g].bitcast(FP8X4),
+                rhs_scale=x_scales[:, t, g],
+                start=first,
+                stop=last,
+            )
+            if last:
                 result = result_pool.tile([P, B, H * W], F32, name="result")
                 nc.scalar.copy(out=result[:].rearrange("p b s -> p (b s)"), in_=acc[ot][:])
                 nc.sync.dma_start(
                     out=out[:, ot * P : (ot + 1) * P].rearrange("b o h w -> o b (h w)"), in_=result[:]
                 )
 
-        for rnd in range(CHUNKS + 2):
-            if rnd < CHUNKS:
+        for rnd in range(UNITS + 3):
+            if rnd < UNITS:
                 flip(rnd)
-            if 0 <= rnd - 1 < CHUNKS:
+            if 0 <= rnd - 1 < UNITS:
                 group(rnd - 1)
-            if 0 <= rnd - 2 < CHUNKS:
-                quantise(rnd - 2)
-            if rnd == X_ROUND:
-                shift_x()
-            if rnd == X_ROUND + 1:
-                quantise_x()
-        for chunk in range(CHUNKS):
-            multiply(chunk)
+            if 0 <= rnd - 3 < UNITS:
+                quantise(rnd - 3)
+        for unit in range(UNITS):
+            multiply(unit)

@@ -22,6 +22,8 @@ CHUNKS = O_TILES * PASSES
 UNITS = CHUNKS * TAPS
 ACC_BANKS = 2
 FLIPPED_BANKS = 8 - ACC_BANKS
+WARM_FIRST, WARM_BEHIND = 4, (3, 7, 11)
+MULTIPLY_LAG = 8
 VECTOR_EVERY = 5
 
 FLOPS = 2 * PIXELS * C_OUT * C_IN * TAPS
@@ -53,6 +55,8 @@ def tile_skeletonconv_s_kernel(tc, x, weight, dilation, step, out):
             )
             w_raw.append(rows)
 
+        warm = keep.tile([P, P], F32)
+        make_identity(nc, warm[:])
         identity = keep.tile([P, P], BF16)
         make_identity(nc, identity[:])
 
@@ -88,6 +92,11 @@ def tile_skeletonconv_s_kernel(tc, x, weight, dilation, step, out):
         w_codes = keep.tile([P, UNITS, P], U32, align_bytes=64)
         w_scales = keep.tile([P, UNITS, P], U8, align_bytes=64)
         w_flipped, w_grouped, acc = {}, {}, {}
+
+        def warm_up(count):
+            for turn in range(count):
+                scratch = flipped_pool.tile([P, P], F32, name="flipped")
+                nc.tensor.matmul(scratch[:], lhsT=warm[:], rhs=warm[:], start=True, stop=True)
 
         def flip(unit):
             chunk, t = divmod(unit, TAPS)
@@ -132,12 +141,18 @@ def tile_skeletonconv_s_kernel(tc, x, weight, dilation, step, out):
                     out=out[:, ot * P : (ot + 1) * P].rearrange("b o h w -> o b (h w)"), in_=result[:]
                 )
 
+        warm_up(WARM_FIRST)
         for rnd in range(UNITS + 3):
             if rnd < UNITS:
                 flip(rnd)
+                if rnd in WARM_BEHIND:
+                    warm_up(1)
             if 0 <= rnd - 1 < UNITS:
                 group(rnd - 1)
             if 0 <= rnd - 3 < UNITS:
                 quantise(rnd - 3)
-        for unit in range(UNITS):
+            if rnd >= MULTIPLY_LAG and (rnd - MULTIPLY_LAG) % TAPS == 0:
+                for unit in range(rnd - MULTIPLY_LAG, rnd - MULTIPLY_LAG + TAPS):
+                    multiply(unit)
+        for unit in range(UNITS - TAPS, UNITS):
             multiply(unit)

@@ -19,12 +19,13 @@ PIXELS = B * H * W
 PASSES = C_IN // K_PASS
 O_TILES = C_OUT // P
 CHUNKS = O_TILES * PASSES
-UNITS = CHUNKS * TAPS
+SORTED = (2, 1, 2, 1, 2, 2)
+WORDS = PACK // 2
 ACC_BANKS = 2
-FLIPPED_BANKS = 8 - ACC_BANKS
-WARM_FIRST, WARM_BEHIND = 4, (3, 7, 11)
-MULTIPLY_LAG = 8
-VECTOR_EVERY = 5
+FIRST_PIECES = 2
+X_CHUNK = 2
+MULTIPLY_LAG = 4
+WARM_FIRST, WARM_ROUNDS = 4, 3
 
 FLOPS = 2 * PIXELS * C_OUT * C_IN * TAPS
 
@@ -34,125 +35,175 @@ def tile_skeletonconv_s_kernel(tc, x, weight, dilation, step, out):
     with ExitStack() as ctx:
         keep = ctx.enter_context(tc.tile_pool(name="keep", bufs=1))
         raw_pool = ctx.enter_context(tc.tile_pool(name="raw", bufs=CHUNKS))
-        grouped_pool = ctx.enter_context(tc.tile_pool(name="grouped", bufs=6))
-        result_pool = ctx.enter_context(tc.tile_pool(name="result", bufs=O_TILES))
-        flipped_pool = ctx.enter_context(tc.psum_pool(name="flipped", bufs=FLIPPED_BANKS))
+        stage = ctx.enter_context(tc.tile_pool(name="stage", bufs=4))
+        flipped_pool = ctx.enter_context(tc.psum_pool(name="flipped", bufs=(8 - ACC_BANKS) // 2))
         acc_pool = ctx.enter_context(tc.psum_pool(name="acc", bufs=ACC_BANKS))
         ctx.enter_context(tc.manual_schedule())
 
         x_raw = keep.tile([P, B, PASSES, PACK, H * W], BF16)
-        nc.sync.dma_start(
-            out=x_raw[:].rearrange("p b g v s -> p (b g) (v s)"),
-            in_=x.rearrange("b (g p v) h w -> p (b g) (v h w)", g=PASSES, v=PACK, p=P),
-        )
         w_raw = []
         for chunk in range(CHUNKS):
+            if chunk == X_CHUNK:
+                nc.sync.dma_start(
+                    out=x_raw[:].rearrange("p b g v s -> p (b g) (v s)"),
+                    in_=x.rearrange("b (g p v) h w -> p (b g) (v h w)", g=PASSES, v=PACK, p=P),
+                )
             ot, g = divmod(chunk, PASSES)
             rows = raw_pool.tile([P, K_PASS * TAPS], BF16, name="rows")
-            nc.sync.dma_start(
-                out=rows[:],
-                in_=weight[ot * P : (ot + 1) * P, g * K_PASS : (g + 1) * K_PASS].rearrange("o c t -> o (c t)"),
-            )
+            width = K_PASS // FIRST_PIECES if chunk == 0 else K_PASS
+            for first in range(0, K_PASS, width):
+                nc.sync.dma_start(
+                    out=rows[:, first * TAPS : (first + width) * TAPS],
+                    in_=weight[
+                        ot * P : (ot + 1) * P, g * K_PASS + first : g * K_PASS + first + width
+                    ].rearrange("o c t -> o (c t)"),
+                )
             w_raw.append(rows)
 
-        warm = keep.tile([P, P], F32)
-        make_identity(nc, warm[:])
+        word_identity = keep.tile([P, P], F32)
+        make_identity(nc, word_identity[:])
         identity = keep.tile([P, P], BF16)
         make_identity(nc, identity[:])
 
-        x_taps = keep.tile([P, TAPS, PASSES, B, H, W, PACK], BF16, align_bytes=64)
-        x_codes = keep.tile([P, TAPS, PASSES, PIXELS], U32, align_bytes=64)
-        x_scales = keep.tile([P, TAPS, PASSES, PIXELS], U8, align_bytes=64)
+        x_grouped = keep.tile([P, PASSES, B, H * W, PACK], BF16, align_bytes=64)
+        x_codes = keep.tile([P, TAPS, PASSES, B, H, W], U32, align_bytes=64)
+        x_scales = keep.tile([P, TAPS, PASSES, B, H, W], U8, align_bytes=64)
+        nc.vector.memset(x_codes[:].rearrange("p t g b h w -> p (t g b h w)").bitcast(I32), 0)
+        nc.vector.memset(x_scales[:].rearrange("p t g b h w -> p (t g b h w)").bitcast(I32), 0)
         centre = TAPS // 2
-        for t in range(TAPS):
-            if t != centre:
-                nc.vector.memset(x_taps[:, t].rearrange("p g b h w v -> p (g b h w v)").bitcast(I32), 0)
-        for g in range(PASSES):
-            nc.vector.tensor_copy(
-                out=x_taps[:, centre, g].rearrange("p b h w v -> p b (h w) v"),
-                in_=x_raw[:, :, g].rearrange("p b v s -> p b s v"),
-            )
-        for t in range(TAPS):
-            if t == centre:
-                continue
-            dh, dw = (t - centre) * step, (t - centre) * dilation
-            h_lo, h_hi = max(0, -dh), H - max(0, dh)
-            w_lo, w_hi = max(0, -dw), W - max(0, dw)
-            nc.vector.tensor_copy(
-                out=x_taps[:, t, :, :, h_lo:h_hi, w_lo:w_hi, :],
-                in_=x_taps[:, centre, :, :, h_lo + dh : h_hi + dh, w_lo + dw : w_hi + dw, :],
-            )
-        for t in (centre, *(t for t in range(TAPS) if t != centre)):
+
+        def group_x():
+            for g in range(PASSES):
+                nc.vector.tensor_copy(
+                    out=x_grouped[:, g], in_=x_raw[:, :, g].rearrange("p b v s -> p b s v")
+                )
+
+        def quantise_x():
             nc.vector.quantize_mx(
-                out=x_codes[:, t].rearrange("p g n -> p (g n)").bitcast(FP8X4),
-                scales=x_scales[:, t].rearrange("p g n -> p (g n)"),
-                in_=x_taps[:, t].rearrange("p g b h w v -> p (g b h w v)"),
+                out=x_codes[:, centre].rearrange("p g b h w -> p (g b h w)").bitcast(FP8X4),
+                scales=x_scales[:, centre].rearrange("p g b h w -> p (g b h w)"),
+                in_=x_grouped[:].rearrange("p g b s v -> p (g b s v)"),
             )
 
-        w_codes = keep.tile([P, UNITS, P], U32, align_bytes=64)
-        w_scales = keep.tile([P, UNITS, P], U8, align_bytes=64)
-        w_flipped, w_grouped, acc = {}, {}, {}
+        def shift_x(plane):
+            for t in range(TAPS):
+                if t == centre:
+                    continue
+                dh, dw = (t - centre) * step, (t - centre) * dilation
+                h_lo, h_hi = max(0, -dh), H - max(0, dh)
+                w_lo, w_hi = max(0, -dw), W - max(0, dw)
+                nc.vector.tensor_copy(
+                    out=plane[:, t, :, :, h_lo:h_hi, w_lo:w_hi],
+                    in_=plane[:, centre, :, :, h_lo + dh : h_hi + dh, w_lo + dw : w_hi + dw],
+                )
+
+        w_codes = keep.tile([P, CHUNKS, TAPS, P], U32, align_bytes=64)
+        w_scales = keep.tile([P, CHUNKS, TAPS, P], U8, align_bytes=64)
+        w_sorted, w_flipped, w_grouped, acc = {}, {}, {}, {}
+
+        def sort(chunk):
+            by_tap = w_raw[chunk][:].rearrange("o (p u h t) -> o t u p h", u=WORDS, h=2, t=TAPS)
+            taps = SORTED[chunk]
+            words = stage.tile([P, taps * WORDS * P * 2], BF16, name="words")
+            by_word = words[:].rearrange("o (t u p h) -> o t u p h", t=taps, u=WORDS, h=2)
+            width = P // FIRST_PIECES if chunk == 0 else P
+            for first in range(0, P, width):
+                piece = slice(first, first + width)
+                if chunk == 0:
+                    for t, copy in enumerate((nc.vector.tensor_copy, nc.scalar.copy)):
+                        copy(out=by_word[:, t, :, piece], in_=by_tap[:, t, :, piece])
+                else:
+                    nc.vector.tensor_copy(out=by_word[:, :, :, piece], in_=by_tap[:, :taps, :, piece])
+            w_sorted[chunk] = words
 
         def warm_up(count):
             for turn in range(count):
-                scratch = flipped_pool.tile([P, P], F32, name="flipped")
-                nc.tensor.matmul(scratch[:], lhsT=warm[:], rhs=warm[:], start=True, stop=True)
+                scratch = acc_pool.tile([P, P], F32, name="acc")
+                nc.tensor.matmul(scratch[:], lhsT=word_identity[:], rhs=word_identity[:], start=True, stop=True)
 
-        def flip(unit):
-            chunk, t = divmod(unit, TAPS)
-            by_value = w_raw[chunk][:].rearrange("o (c v t) -> o t v c", v=PACK, t=TAPS)
-            flipped = flipped_pool.tile([P, PACK, P], BF16, name="flipped")
-            for v in range(PACK):
-                nc.tensor.transpose(flipped[:, v, :], by_value[:, t, v], identity[:])
-            w_flipped[unit] = flipped
+        def flip(chunk):
+            taps = SORTED[chunk]
+            by_value = w_raw[chunk][:].rearrange("o (p v t) -> o t v p", v=PACK, t=TAPS)
+            flipped = flipped_pool.tile([P, TAPS - taps, PACK, P], BF16, name="flipped_values")
+            for t in range(taps, TAPS):
+                for v in range(PACK):
+                    nc.tensor.transpose(flipped[:, t - taps, v, :], by_value[:, t, v], identity[:])
+            w_flipped[chunk, "values"] = flipped
+            flipped = flipped_pool.tile([P, taps, WORDS, P], F32, name="flipped_words")
+            words = w_sorted[chunk][:].bitcast(F32).rearrange("o (t u p) -> o t u p", t=taps, u=WORDS)
+            for t in range(taps):
+                for u in range(WORDS):
+                    nc.tensor.transpose(flipped[:, t, u, :], words[:, t, u], word_identity[:])
+            w_flipped[chunk, "words"] = flipped
 
-        def group(unit):
-            grouped = grouped_pool.tile([P, P, PACK], BF16, name="grouped", align_bytes=64)
-            copy = nc.vector.tensor_copy if unit * 2 % VECTOR_EVERY >= VECTOR_EVERY - 2 else nc.scalar.copy
-            copy(out=grouped[:], in_=w_flipped[unit][:].rearrange("p v o -> p o v"))
-            w_grouped[unit] = grouped
+        def group(chunk):
+            taps = SORTED[chunk]
+            grouped = stage.tile([P, TAPS - taps, P, PACK], BF16, name="grouped_values", align_bytes=64)
+            nc.scalar.copy(out=grouped[:], in_=w_flipped[chunk, "values"][:].rearrange("p t v o -> p t o v"))
+            w_grouped[chunk, "values"] = grouped
+            grouped = stage.tile([P, taps * P * PACK], BF16, name="grouped_words", align_bytes=64)
+            nc.scalar.copy(
+                out=grouped[:].bitcast(F32).rearrange("p (t o u) -> p t o u", t=taps, u=WORDS),
+                in_=w_flipped[chunk, "words"][:].rearrange("p t u o -> p t o u"),
+            )
+            w_grouped[chunk, "words"] = grouped
 
-        def quantise(unit):
+        def quantise_values(chunk):
             nc.vector.quantize_mx(
-                out=w_codes[:, unit].bitcast(FP8X4),
-                scales=w_scales[:, unit],
-                in_=w_grouped[unit][:].rearrange("p o v -> p (o v)"),
+                out=w_codes[:, chunk, SORTED[chunk] :].rearrange("p t o -> p (t o)").bitcast(FP8X4),
+                scales=w_scales[:, chunk, SORTED[chunk] :].rearrange("p t o -> p (t o)"),
+                in_=w_grouped[chunk, "values"][:].rearrange("p t o v -> p (t o v)"),
             )
 
-        def multiply(unit):
-            chunk, t = divmod(unit, TAPS)
-            ot, g = divmod(chunk, PASSES)
-            first, last = g == 0 and t == 0, g == PASSES - 1 and t == TAPS - 1
-            if first:
-                acc[ot] = acc_pool.tile([P, PIXELS], F32, name="acc")
-            nc.tensor.matmul_mx(
-                out=acc[ot][:],
-                lhsT=w_codes[:, unit].bitcast(FP8X4),
-                lhsT_scale=w_scales[:, unit],
-                rhs=x_codes[:, t, g].bitcast(FP8X4),
-                rhs_scale=x_scales[:, t, g],
-                start=first,
-                stop=last,
+        def quantise_words(chunk):
+            nc.vector.quantize_mx(
+                out=w_codes[:, chunk, : SORTED[chunk]].rearrange("p t o -> p (t o)").bitcast(FP8X4),
+                scales=w_scales[:, chunk, : SORTED[chunk]].rearrange("p t o -> p (t o)"),
+                in_=w_grouped[chunk, "words"][:],
             )
-            if last:
-                result = result_pool.tile([P, B, H * W], F32, name="result")
-                nc.scalar.copy(out=result[:].rearrange("p b s -> p (b s)"), in_=acc[ot][:])
-                nc.sync.dma_start(
-                    out=out[:, ot * P : (ot + 1) * P].rearrange("b o h w -> o b (h w)"), in_=result[:]
+
+        def multiply(chunk):
+            ot, g = divmod(chunk, PASSES)
+            if g == 0:
+                acc[ot] = acc_pool.tile([P, PIXELS], F32, name="acc")
+            for t in range(TAPS):
+                nc.tensor.matmul_mx(
+                    out=acc[ot][:],
+                    lhsT=w_codes[:, chunk, t].bitcast(FP8X4),
+                    lhsT_scale=w_scales[:, chunk, t],
+                    rhs=x_codes[:, t, g].rearrange("p b h w -> p (b h w)").bitcast(FP8X4),
+                    rhs_scale=x_scales[:, t, g].rearrange("p b h w -> p (b h w)"),
+                    start=(g == 0 and t == 0),
+                    stop=(g == PASSES - 1 and t == TAPS - 1),
                 )
 
+        def store(ot):
+            result = keep.tile([P, B, H * W], F32, name="result%d" % ot)
+            nc.scalar.copy(out=result[:].rearrange("p b s -> p (b s)"), in_=acc[ot][:])
+            nc.sync.dma_start(out=out[:, ot * P : (ot + 1) * P].rearrange("b o h w -> o b (h w)"), in_=result[:])
+
+        x_steps = {
+            0: group_x,
+            1: quantise_x,
+            2: lambda: shift_x(x_codes[:].bitcast(I32)),
+            3: lambda: shift_x(x_scales[:]),
+        }
         warm_up(WARM_FIRST)
-        for rnd in range(UNITS + 3):
-            if rnd < UNITS:
+        sort(0)
+        for rnd in range(CHUNKS + MULTIPLY_LAG):
+            if rnd + 1 < CHUNKS:
+                sort(rnd + 1)
+            if rnd < CHUNKS:
                 flip(rnd)
-                if rnd in WARM_BEHIND:
-                    warm_up(1)
-            if 0 <= rnd - 1 < UNITS:
-                group(rnd - 1)
-            if 0 <= rnd - 3 < UNITS:
-                quantise(rnd - 3)
-            if rnd >= MULTIPLY_LAG and (rnd - MULTIPLY_LAG) % TAPS == 0:
-                for unit in range(rnd - MULTIPLY_LAG, rnd - MULTIPLY_LAG + TAPS):
-                    multiply(unit)
-        for unit in range(UNITS - TAPS, UNITS):
-            multiply(unit)
+                group(rnd)
+            if rnd < WARM_ROUNDS:
+                warm_up(1)
+            if 0 <= rnd - 1 < CHUNKS:
+                quantise_values(rnd - 1)
+                quantise_words(rnd - 1)
+            if rnd in x_steps:
+                x_steps[rnd]()
+            if 0 <= rnd - MULTIPLY_LAG < CHUNKS:
+                multiply(rnd - MULTIPLY_LAG)
+                if (rnd - MULTIPLY_LAG) % PASSES == PASSES - 1:
+                    store((rnd - MULTIPLY_LAG) // PASSES)

@@ -19,13 +19,14 @@ PIXELS = B * H * W
 PASSES = C_IN // K_PASS
 O_TILES = C_OUT // P
 CHUNKS = O_TILES * PASSES
-SORTED = (2, 1, 2, 1, 2, 2)
+GROUPS = (slice(0, 2), slice(2, 3))
+SCALAR_SORTS = 3
 WORDS = PACK // 2
 ACC_BANKS = 2
 FIRST_PIECES = 2
-X_CHUNK = 2
-MULTIPLY_LAG = 4
-WARM_FIRST, WARM_ROUNDS = 4, 3
+X_CHUNK = 1
+WARMING = 4
+MULTIPLY_LAG = 3
 
 FLOPS = 2 * PIXELS * C_OUT * C_IN * TAPS
 
@@ -36,7 +37,7 @@ def tile_skeletonconv_s_kernel(tc, x, weight, dilation, step, out):
         keep = ctx.enter_context(tc.tile_pool(name="keep", bufs=1))
         raw_pool = ctx.enter_context(tc.tile_pool(name="raw", bufs=CHUNKS))
         stage = ctx.enter_context(tc.tile_pool(name="stage", bufs=4))
-        flipped_pool = ctx.enter_context(tc.psum_pool(name="flipped", bufs=(8 - ACC_BANKS) // 2))
+        flipped_pool = ctx.enter_context(tc.psum_pool(name="flipped", bufs=(8 - ACC_BANKS) // len(GROUPS)))
         acc_pool = ctx.enter_context(tc.psum_pool(name="acc", bufs=ACC_BANKS))
         ctx.enter_context(tc.manual_schedule())
 
@@ -60,9 +61,7 @@ def tile_skeletonconv_s_kernel(tc, x, weight, dilation, step, out):
                 )
             w_raw.append(rows)
 
-        word_identity = keep.tile([P, P], F32)
-        make_identity(nc, word_identity[:])
-        identity = keep.tile([P, P], BF16)
+        identity = keep.tile([P, P], F32)
         make_identity(nc, identity[:])
 
         x_grouped = keep.tile([P, PASSES, B, H * W, PACK], BF16, align_bytes=64)
@@ -73,10 +72,8 @@ def tile_skeletonconv_s_kernel(tc, x, weight, dilation, step, out):
         centre = TAPS // 2
 
         def group_x():
-            for g in range(PASSES):
-                nc.vector.tensor_copy(
-                    out=x_grouped[:, g], in_=x_raw[:, :, g].rearrange("p b v s -> p b s v")
-                )
+            for g, copy in enumerate((nc.vector.tensor_copy, nc.scalar.copy)):
+                copy(out=x_grouped[:, g], in_=x_raw[:, :, g].rearrange("p b v s -> p b s v"))
 
         def quantise_x():
             nc.vector.quantize_mx(
@@ -101,66 +98,52 @@ def tile_skeletonconv_s_kernel(tc, x, weight, dilation, step, out):
         w_scales = keep.tile([P, CHUNKS, TAPS, P], U8, align_bytes=64)
         w_sorted, w_flipped, w_grouped, acc = {}, {}, {}, {}
 
-        def sort(chunk):
-            by_tap = w_raw[chunk][:].rearrange("o (p u h t) -> o t u p h", u=WORDS, h=2, t=TAPS)
-            taps = SORTED[chunk]
-            words = stage.tile([P, taps * WORDS * P * 2], BF16, name="words")
-            by_word = words[:].rearrange("o (t u p h) -> o t u p h", t=taps, u=WORDS, h=2)
+        def sort(chunk, engine):
+            by_tap = w_raw[chunk][:].rearrange("o (p u h t) -> o t p u h", u=WORDS, h=2, t=TAPS)
+            if chunk not in w_sorted:
+                words = stage.tile([P, TAPS * WORDS * P * 2], BF16, name="words")
+                w_sorted[chunk] = words
+            by_word = w_sorted[chunk][:].rearrange("o (t u p h) -> o t p u h", t=TAPS, u=WORDS, h=2)
             width = P // FIRST_PIECES if chunk == 0 else P
             for first in range(0, P, width):
                 piece = slice(first, first + width)
-                if chunk == 0:
-                    for t, copy in enumerate((nc.vector.tensor_copy, nc.scalar.copy)):
-                        copy(out=by_word[:, t, :, piece], in_=by_tap[:, t, :, piece])
-                else:
-                    nc.vector.tensor_copy(out=by_word[:, :, :, piece], in_=by_tap[:, :taps, :, piece])
-            w_sorted[chunk] = words
+                for group, taps in enumerate(GROUPS):
+                    scalar_sorts = group == 1 and chunk < SCALAR_SORTS
+                    if engine == "scalar" and scalar_sorts:
+                        nc.scalar.copy(out=by_word[:, taps, piece], in_=by_tap[:, taps, piece])
+                    if engine == "vector" and not scalar_sorts:
+                        nc.vector.tensor_copy(out=by_word[:, taps, piece], in_=by_tap[:, taps, piece])
 
-        def warm_up(count):
-            for turn in range(count):
+        def warm_up():
+            for turn in range(WARMING):
                 scratch = acc_pool.tile([P, P], F32, name="acc")
-                nc.tensor.matmul(scratch[:], lhsT=word_identity[:], rhs=word_identity[:], start=True, stop=True)
+                nc.tensor.matmul(scratch[:], lhsT=identity[:], rhs=identity[:], start=True, stop=True)
 
         def flip(chunk):
-            taps = SORTED[chunk]
-            by_value = w_raw[chunk][:].rearrange("o (p v t) -> o t v p", v=PACK, t=TAPS)
-            flipped = flipped_pool.tile([P, TAPS - taps, PACK, P], BF16, name="flipped_values")
-            for t in range(taps, TAPS):
-                for v in range(PACK):
-                    nc.tensor.transpose(flipped[:, t - taps, v, :], by_value[:, t, v], identity[:])
-            w_flipped[chunk, "values"] = flipped
-            flipped = flipped_pool.tile([P, taps, WORDS, P], F32, name="flipped_words")
-            words = w_sorted[chunk][:].bitcast(F32).rearrange("o (t u p) -> o t u p", t=taps, u=WORDS)
-            for t in range(taps):
-                for u in range(WORDS):
-                    nc.tensor.transpose(flipped[:, t, u, :], words[:, t, u], word_identity[:])
-            w_flipped[chunk, "words"] = flipped
+            words = w_sorted[chunk][:].bitcast(F32).rearrange("o (t u p) -> o t u p", t=TAPS, u=WORDS)
+            for group, taps in enumerate(GROUPS):
+                flipped = flipped_pool.tile([P, taps.stop - taps.start, WORDS, P], F32, name="flipped%d" % group)
+                for t in range(taps.start, taps.stop):
+                    for u in range(WORDS):
+                        nc.tensor.transpose(flipped[:, t - taps.start, u, :], words[:, t, u], identity[:])
+                w_flipped[chunk, group] = flipped
 
-        def group(chunk):
-            taps = SORTED[chunk]
-            grouped = stage.tile([P, TAPS - taps, P, PACK], BF16, name="grouped_values", align_bytes=64)
-            nc.scalar.copy(out=grouped[:], in_=w_flipped[chunk, "values"][:].rearrange("p t v o -> p t o v"))
-            w_grouped[chunk, "values"] = grouped
-            grouped = stage.tile([P, taps * P * PACK], BF16, name="grouped_words", align_bytes=64)
+        def gather(chunk, group):
+            count = GROUPS[group].stop - GROUPS[group].start
+            grouped = stage.tile([P, count * P * PACK], BF16, name="grouped%d" % group, align_bytes=64)
             nc.scalar.copy(
-                out=grouped[:].bitcast(F32).rearrange("p (t o u) -> p t o u", t=taps, u=WORDS),
-                in_=w_flipped[chunk, "words"][:].rearrange("p t u o -> p t o u"),
+                out=grouped[:].bitcast(F32).rearrange("p (t o u) -> p t o u", t=count, u=WORDS),
+                in_=w_flipped[chunk, group][:].rearrange("p t u o -> p t o u"),
             )
-            w_grouped[chunk, "words"] = grouped
+            w_grouped[chunk, group] = grouped
 
-        def quantise_values(chunk):
-            nc.vector.quantize_mx(
-                out=w_codes[:, chunk, SORTED[chunk] :].rearrange("p t o -> p (t o)").bitcast(FP8X4),
-                scales=w_scales[:, chunk, SORTED[chunk] :].rearrange("p t o -> p (t o)"),
-                in_=w_grouped[chunk, "values"][:].rearrange("p t o v -> p (t o v)"),
-            )
-
-        def quantise_words(chunk):
-            nc.vector.quantize_mx(
-                out=w_codes[:, chunk, : SORTED[chunk]].rearrange("p t o -> p (t o)").bitcast(FP8X4),
-                scales=w_scales[:, chunk, : SORTED[chunk]].rearrange("p t o -> p (t o)"),
-                in_=w_grouped[chunk, "words"][:],
-            )
+        def quantise(chunk):
+            for group, taps in enumerate(GROUPS):
+                nc.vector.quantize_mx(
+                    out=w_codes[:, chunk, taps].rearrange("p t o -> p (t o)").bitcast(FP8X4),
+                    scales=w_scales[:, chunk, taps].rearrange("p t o -> p (t o)"),
+                    in_=w_grouped[chunk, group][:],
+                )
 
         def multiply(chunk):
             ot, g = divmod(chunk, PASSES)
@@ -183,24 +166,26 @@ def tile_skeletonconv_s_kernel(tc, x, weight, dilation, step, out):
             nc.sync.dma_start(out=out[:, ot * P : (ot + 1) * P].rearrange("b o h w -> o b (h w)"), in_=result[:])
 
         x_steps = {
-            0: group_x,
-            1: quantise_x,
-            2: lambda: shift_x(x_codes[:].bitcast(I32)),
-            3: lambda: shift_x(x_scales[:]),
+            0: quantise_x,
+            1: lambda: shift_x(x_codes[:].bitcast(I32)),
+            2: lambda: shift_x(x_scales[:]),
         }
-        warm_up(WARM_FIRST)
-        sort(0)
+        warm_up()
+        sort(0, "vector")
+        sort(0, "scalar")
+        group_x()
         for rnd in range(CHUNKS + MULTIPLY_LAG):
             if rnd + 1 < CHUNKS:
-                sort(rnd + 1)
+                sort(rnd + 1, "vector")
             if rnd < CHUNKS:
                 flip(rnd)
-                group(rnd)
-            if rnd < WARM_ROUNDS:
-                warm_up(1)
+                gather(rnd, 0)
+            if rnd + 1 < CHUNKS:
+                sort(rnd + 1, "scalar")
+            if rnd < CHUNKS:
+                gather(rnd, 1)
             if 0 <= rnd - 1 < CHUNKS:
-                quantise_values(rnd - 1)
-                quantise_words(rnd - 1)
+                quantise(rnd - 1)
             if rnd in x_steps:
                 x_steps[rnd]()
             if 0 <= rnd - MULTIPLY_LAG < CHUNKS:

@@ -20,13 +20,13 @@ PASSES = C_IN // K_PASS
 O_TILES = C_OUT // P
 CHUNKS = O_TILES * PASSES
 GROUPS = (slice(0, 2), slice(2, 3))
-SCALAR_SORTS = 3
+SCALAR_SORTS = 4
 WORDS = PACK // 2
-ACC_BANKS = 2
-FIRST_PIECES = 2
-X_CHUNK = 1
+FLIPPED_BANKS = (3, 2)
+PIECES = (2, 2, 1, 1, 1, 1)
 WARMING = 4
-MULTIPLY_LAG = 3
+SORT_LEAD = 2
+MULTIPLY_LAG = 4
 
 FLOPS = 2 * PIXELS * C_OUT * C_IN * TAPS
 
@@ -37,21 +37,20 @@ def tile_skeletonconv_s_kernel(tc, x, weight, dilation, step, out):
         keep = ctx.enter_context(tc.tile_pool(name="keep", bufs=1))
         raw_pool = ctx.enter_context(tc.tile_pool(name="raw", bufs=CHUNKS))
         stage = ctx.enter_context(tc.tile_pool(name="stage", bufs=4))
-        flipped_pool = ctx.enter_context(tc.psum_pool(name="flipped", bufs=(8 - ACC_BANKS) // len(GROUPS)))
-        acc_pool = ctx.enter_context(tc.psum_pool(name="acc", bufs=ACC_BANKS))
+        flipped_pool = ctx.enter_context(tc.psum_pool(name="flipped", bufs=1))
+        acc_pool = ctx.enter_context(tc.psum_pool(name="acc", bufs=O_TILES))
         ctx.enter_context(tc.manual_schedule())
 
         x_raw = keep.tile([P, B, PASSES, PACK, H * W], BF16)
+        nc.sync.dma_start(
+            out=x_raw[:].rearrange("p b g v s -> p (b g) (v s)"),
+            in_=x.rearrange("b (g p v) h w -> p (b g) (v h w)", g=PASSES, v=PACK, p=P),
+        )
         w_raw = []
         for chunk in range(CHUNKS):
-            if chunk == X_CHUNK:
-                nc.sync.dma_start(
-                    out=x_raw[:].rearrange("p b g v s -> p (b g) (v s)"),
-                    in_=x.rearrange("b (g p v) h w -> p (b g) (v h w)", g=PASSES, v=PACK, p=P),
-                )
             ot, g = divmod(chunk, PASSES)
             rows = raw_pool.tile([P, K_PASS * TAPS], BF16, name="rows")
-            width = K_PASS // FIRST_PIECES if chunk == 0 else K_PASS
+            width = K_PASS // PIECES[chunk]
             for first in range(0, K_PASS, width):
                 nc.sync.dma_start(
                     out=rows[:, first * TAPS : (first + width) * TAPS],
@@ -72,8 +71,8 @@ def tile_skeletonconv_s_kernel(tc, x, weight, dilation, step, out):
         centre = TAPS // 2
 
         def group_x():
-            for g, copy in enumerate((nc.vector.tensor_copy, nc.scalar.copy)):
-                copy(out=x_grouped[:, g], in_=x_raw[:, :, g].rearrange("p b v s -> p b s v"))
+            for g in range(PASSES):
+                nc.vector.tensor_copy(out=x_grouped[:, g], in_=x_raw[:, :, g].rearrange("p b v s -> p b s v"))
 
         def quantise_x():
             nc.vector.quantize_mx(
@@ -104,7 +103,7 @@ def tile_skeletonconv_s_kernel(tc, x, weight, dilation, step, out):
                 words = stage.tile([P, TAPS * WORDS * P * 2], BF16, name="words")
                 w_sorted[chunk] = words
             by_word = w_sorted[chunk][:].rearrange("o (t u p h) -> o t p u h", t=TAPS, u=WORDS, h=2)
-            width = P // FIRST_PIECES if chunk == 0 else P
+            width = P // PIECES[chunk]
             for first in range(0, P, width):
                 piece = slice(first, first + width)
                 for group, taps in enumerate(GROUPS):
@@ -122,7 +121,9 @@ def tile_skeletonconv_s_kernel(tc, x, weight, dilation, step, out):
         def flip(chunk):
             words = w_sorted[chunk][:].bitcast(F32).rearrange("o (t u p) -> o t u p", t=TAPS, u=WORDS)
             for group, taps in enumerate(GROUPS):
-                flipped = flipped_pool.tile([P, taps.stop - taps.start, WORDS, P], F32, name="flipped%d" % group)
+                flipped = flipped_pool.tile(
+                    [P, taps.stop - taps.start, WORDS, P], F32, name="flipped%d" % group, bufs=FLIPPED_BANKS[group]
+                )
                 for t in range(taps.start, taps.stop):
                     for u in range(WORDS):
                         nc.tensor.transpose(flipped[:, t - taps.start, u, :], words[:, t, u], identity[:])
@@ -165,29 +166,27 @@ def tile_skeletonconv_s_kernel(tc, x, weight, dilation, step, out):
             nc.scalar.copy(out=result[:].rearrange("p b s -> p (b s)"), in_=acc[ot][:])
             nc.sync.dma_start(out=out[:, ot * P : (ot + 1) * P].rearrange("b o h w -> o b (h w)"), in_=result[:])
 
-        x_steps = {
-            0: quantise_x,
-            1: lambda: shift_x(x_codes[:].bitcast(I32)),
-            2: lambda: shift_x(x_scales[:]),
-        }
         warm_up()
+        group_x()
         sort(0, "vector")
         sort(0, "scalar")
-        group_x()
+        quantise_x()
+        sort(1, "vector")
+        sort(1, "scalar")
+        shift_x(x_codes[:].bitcast(I32))
         for rnd in range(CHUNKS + MULTIPLY_LAG):
-            if rnd + 1 < CHUNKS:
-                sort(rnd + 1, "vector")
+            if rnd + SORT_LEAD < CHUNKS:
+                sort(rnd + SORT_LEAD, "vector")
+            if rnd == 0:
+                shift_x(x_scales[:])
             if rnd < CHUNKS:
                 flip(rnd)
-                gather(rnd, 0)
-            if rnd + 1 < CHUNKS:
-                sort(rnd + 1, "scalar")
-            if rnd < CHUNKS:
-                gather(rnd, 1)
+                for group in range(len(GROUPS)):
+                    gather(rnd, group)
+            if rnd + SORT_LEAD < CHUNKS:
+                sort(rnd + SORT_LEAD, "scalar")
             if 0 <= rnd - 1 < CHUNKS:
                 quantise(rnd - 1)
-            if rnd in x_steps:
-                x_steps[rnd]()
             if 0 <= rnd - MULTIPLY_LAG < CHUNKS:
                 multiply(rnd - MULTIPLY_LAG)
                 if (rnd - MULTIPLY_LAG) % PASSES == PASSES - 1:

@@ -24,7 +24,7 @@ SCALAR_SORTS = 4
 WORDS = PACK // 2
 FLIPPED_BANKS = (3, 2)
 PIECES = (2, 2, 1, 1, 1, 1)
-WARMING = 4
+WARMING, WARM_ROUNDS = 4, (0, 1, 2)
 SORT_LEAD = 2
 MULTIPLY_LAG = 4
 
@@ -71,8 +71,8 @@ def tile_skeletonconv_s_kernel(tc, x, weight, dilation, step, out):
         centre = TAPS // 2
 
         def group_x():
-            for g in range(PASSES):
-                nc.vector.tensor_copy(out=x_grouped[:, g], in_=x_raw[:, :, g].rearrange("p b v s -> p b s v"))
+            for g, copy in enumerate((nc.vector.tensor_copy, nc.scalar.copy)):
+                copy(out=x_grouped[:, g], in_=x_raw[:, :, g].rearrange("p b v s -> p b s v"))
 
         def quantise_x():
             nc.vector.quantize_mx(
@@ -113,8 +113,8 @@ def tile_skeletonconv_s_kernel(tc, x, weight, dilation, step, out):
                     if engine == "vector" and not scalar_sorts:
                         nc.vector.tensor_copy(out=by_word[:, taps, piece], in_=by_tap[:, taps, piece])
 
-        def warm_up():
-            for turn in range(WARMING):
+        def warm_up(count):
+            for turn in range(count):
                 scratch = acc_pool.tile([P, P], F32, name="acc")
                 nc.tensor.matmul(scratch[:], lhsT=identity[:], rhs=identity[:], start=True, stop=True)
 
@@ -166,7 +166,7 @@ def tile_skeletonconv_s_kernel(tc, x, weight, dilation, step, out):
             nc.scalar.copy(out=result[:].rearrange("p b s -> p (b s)"), in_=acc[ot][:])
             nc.sync.dma_start(out=out[:, ot * P : (ot + 1) * P].rearrange("b o h w -> o b (h w)"), in_=result[:])
 
-        warm_up()
+        warm_up(WARMING)
         group_x()
         sort(0, "vector")
         sort(0, "scalar")
@@ -174,13 +174,14 @@ def tile_skeletonconv_s_kernel(tc, x, weight, dilation, step, out):
         sort(1, "vector")
         sort(1, "scalar")
         shift_x(x_codes[:].bitcast(I32))
+        shift_x(x_scales[:])
         for rnd in range(CHUNKS + MULTIPLY_LAG):
             if rnd + SORT_LEAD < CHUNKS:
                 sort(rnd + SORT_LEAD, "vector")
-            if rnd == 0:
-                shift_x(x_scales[:])
             if rnd < CHUNKS:
                 flip(rnd)
+                if rnd in WARM_ROUNDS:
+                    warm_up(1)
                 for group in range(len(GROUPS)):
                     gather(rnd, group)
             if rnd + SORT_LEAD < CHUNKS:

@@ -26,7 +26,12 @@ FLIPPED_BANKS = (3, 2)
 PIECES = (2, 2, 1, 1, 1, 1)
 WARMING, WARM_ROUNDS = 4, (0, 1, 2)
 SORT_LEAD = 2
-MULTIPLY_LAG = 4
+QUANTISED = {
+    3: ((0, 0, 4), (0, 4, 6)),
+    5: ((1, 0, 4), (1, 4, 6), (2, 0, 2), (2, 2, 3)),
+    6: ((2, 3, 5), (2, 5, 6)),
+}
+MULTIPLY_LAG = 5
 
 FLOPS = 2 * PIXELS * C_OUT * C_IN * TAPS
 
@@ -93,8 +98,8 @@ def tile_skeletonconv_s_kernel(tc, x, weight, dilation, step, out):
                     in_=plane[:, centre, :, :, h_lo + dh : h_hi + dh, w_lo + dw : w_hi + dw],
                 )
 
-        w_codes = keep.tile([P, CHUNKS, TAPS, P], U32, align_bytes=64)
-        w_scales = keep.tile([P, CHUNKS, TAPS, P], U8, align_bytes=64)
+        w_codes = keep.tile([P, CHUNKS * TAPS, P], U32, align_bytes=64)
+        w_scales = keep.tile([P, CHUNKS * TAPS, P], U8, align_bytes=64)
         w_sorted, w_flipped, w_grouped, acc = {}, {}, {}, {}
 
         def sort(chunk, engine):
@@ -130,21 +135,23 @@ def tile_skeletonconv_s_kernel(tc, x, weight, dilation, step, out):
                 w_flipped[chunk, group] = flipped
 
         def gather(chunk, group):
-            count = GROUPS[group].stop - GROUPS[group].start
-            grouped = stage.tile([P, count * P * PACK], BF16, name="grouped%d" % group, align_bytes=64)
+            ot, g = divmod(chunk, PASSES)
+            if ot not in w_grouped:
+                grouped = stage.tile([P, PASSES * TAPS, P * PACK], BF16, name="grouped", align_bytes=64)
+                w_grouped[ot] = grouped
+            units = w_grouped[ot][:, g * TAPS + GROUPS[group].start : g * TAPS + GROUPS[group].stop]
             nc.scalar.copy(
-                out=grouped[:].bitcast(F32).rearrange("p (t o u) -> p t o u", t=count, u=WORDS),
+                out=units.bitcast(F32).rearrange("p t (o u) -> p t o u", u=WORDS),
                 in_=w_flipped[chunk, group][:].rearrange("p t u o -> p t o u"),
             )
-            w_grouped[chunk, group] = grouped
 
-        def quantise(chunk):
-            for group, taps in enumerate(GROUPS):
-                nc.vector.quantize_mx(
-                    out=w_codes[:, chunk, taps].rearrange("p t o -> p (t o)").bitcast(FP8X4),
-                    scales=w_scales[:, chunk, taps].rearrange("p t o -> p (t o)"),
-                    in_=w_grouped[chunk, group][:],
-                )
+        def quantise(ot, first, last):
+            units = slice(ot * PASSES * TAPS + first, ot * PASSES * TAPS + last)
+            nc.vector.quantize_mx(
+                out=w_codes[:, units].rearrange("p i o -> p (i o)").bitcast(FP8X4),
+                scales=w_scales[:, units].rearrange("p i o -> p (i o)"),
+                in_=w_grouped[ot][:, first:last].rearrange("p i n -> p (i n)"),
+            )
 
         def multiply(chunk):
             ot, g = divmod(chunk, PASSES)
@@ -153,8 +160,8 @@ def tile_skeletonconv_s_kernel(tc, x, weight, dilation, step, out):
             for t in range(TAPS):
                 nc.tensor.matmul_mx(
                     out=acc[ot][:],
-                    lhsT=w_codes[:, chunk, t].bitcast(FP8X4),
-                    lhsT_scale=w_scales[:, chunk, t],
+                    lhsT=w_codes[:, chunk * TAPS + t].bitcast(FP8X4),
+                    lhsT_scale=w_scales[:, chunk * TAPS + t],
                     rhs=x_codes[:, t, g].rearrange("p b h w -> p (b h w)").bitcast(FP8X4),
                     rhs_scale=x_scales[:, t, g].rearrange("p b h w -> p (b h w)"),
                     start=(g == 0 and t == 0),
@@ -186,8 +193,8 @@ def tile_skeletonconv_s_kernel(tc, x, weight, dilation, step, out):
                     gather(rnd, group)
             if rnd + SORT_LEAD < CHUNKS:
                 sort(rnd + SORT_LEAD, "scalar")
-            if 0 <= rnd - 1 < CHUNKS:
-                quantise(rnd - 1)
+            for ot, first, last in QUANTISED.get(rnd, ()):
+                quantise(ot, first, last)
             if 0 <= rnd - MULTIPLY_LAG < CHUNKS:
                 multiply(rnd - MULTIPLY_LAG)
                 if (rnd - MULTIPLY_LAG) % PASSES == PASSES - 1:

from contextlib import ExitStack

import concourse.mybir as mybir
from concourse.masks import make_identity

BF16 = mybir.dt.bfloat16
F32 = mybir.dt.float32
I32 = mybir.dt.int32
U32 = mybir.dt.uint32
U8 = mybir.dt.uint8
FP8X4 = mybir.dt.float8_e4m3fn_x4

P = 128
PACK = 4
K_PASS = P * PACK

B, C_IN, C_OUT, TAPS, H, W = 2, 1024, 384, 3, 8, 8
PIXELS = B * H * W
PASSES = C_IN // K_PASS
O_TILES = C_OUT // P
CHUNKS = O_TILES * PASSES
GROUPS = (slice(0, 2), slice(2, 3))
SCALAR_SORTS = 4
WORDS = PACK // 2
FLIPPED_BANKS = (3, 2)
PIECES = (2, 2, 1, 1, 1, 1)
WARMING, WARM_ROUNDS = 4, (0, 1, 2)
SORT_LEAD = 2
QUANTISED = {
    3: ((0, 0, 4), (0, 4, 6)),
    5: ((1, 0, 4), (1, 4, 6), (2, 0, 2), (2, 2, 3)),
    6: ((2, 3, 5), (2, 5, 6)),
}
MULTIPLY_LAG = 5

FLOPS = 2 * PIXELS * C_OUT * C_IN * TAPS


def tile_skeletonconv_s_kernel(tc, x, weight, dilation, step, out):
    nc = tc.nc
    with ExitStack() as ctx:
        keep = ctx.enter_context(tc.tile_pool(name="keep", bufs=1))
        raw_pool = ctx.enter_context(tc.tile_pool(name="raw", bufs=CHUNKS))
        stage = ctx.enter_context(tc.tile_pool(name="stage", bufs=4))
        flipped_pool = ctx.enter_context(tc.psum_pool(name="flipped", bufs=1))
        acc_pool = ctx.enter_context(tc.psum_pool(name="acc", bufs=O_TILES))
        ctx.enter_context(tc.manual_schedule())

        x_raw = keep.tile([P, B, PASSES, PACK, H * W], BF16)
        nc.sync.dma_start(
            out=x_raw[:].rearrange("p b g v s -> p (b g) (v s)"),
            in_=x.rearrange("b (g p v) h w -> p (b g) (v h w)", g=PASSES, v=PACK, p=P),
        )
        w_raw = []
        for chunk in range(CHUNKS):
            ot, g = divmod(chunk, PASSES)
            rows = raw_pool.tile([P, K_PASS * TAPS], BF16, name="rows")
            width = K_PASS // PIECES[chunk]
            for first in range(0, K_PASS, width):
                nc.sync.dma_start(
                    out=rows[:, first * TAPS : (first + width) * TAPS],
                    in_=weight[
                        ot * P : (ot + 1) * P, g * K_PASS + first : g * K_PASS + first + width
                    ].rearrange("o c t -> o (c t)"),
                )
            w_raw.append(rows)

        identity = keep.tile([P, P], F32)
        make_identity(nc, identity[:])

        x_grouped = keep.tile([P, PASSES, B, H * W, PACK], BF16, align_bytes=64)
        x_codes = keep.tile([P, TAPS, PASSES, B, H, W], U32, align_bytes=64)
        x_scales = keep.tile([P, TAPS, PASSES, B, H, W], U8, align_bytes=64)
        nc.vector.memset(x_codes[:].rearrange("p t g b h w -> p (t g b h w)").bitcast(I32), 0)
        nc.vector.memset(x_scales[:].rearrange("p t g b h w -> p (t g b h w)").bitcast(I32), 0)
        centre = TAPS // 2

        def group_x():
            for g, copy in enumerate((nc.vector.tensor_copy, nc.scalar.copy)):
                copy(out=x_grouped[:, g], in_=x_raw[:, :, g].rearrange("p b v s -> p b s v"))

        def quantise_x():
            nc.vector.quantize_mx(
                out=x_codes[:, centre].rearrange("p g b h w -> p (g b h w)").bitcast(FP8X4),
                scales=x_scales[:, centre].rearrange("p g b h w -> p (g b h w)"),
                in_=x_grouped[:].rearrange("p g b s v -> p (g b s v)"),
            )

        def shift_x(plane):
            for t in range(TAPS):
                if t == centre:
                    continue
                dh, dw = (t - centre) * step, (t - centre) * dilation
                h_lo, h_hi = max(0, -dh), H - max(0, dh)
                w_lo, w_hi = max(0, -dw), W - max(0, dw)
                nc.vector.tensor_copy(
                    out=plane[:, t, :, :, h_lo:h_hi, w_lo:w_hi],
                    in_=plane[:, centre, :, :, h_lo + dh : h_hi + dh, w_lo + dw : w_hi + dw],
                )

        w_codes = keep.tile([P, CHUNKS * TAPS, P], U32, align_bytes=64)
        w_scales = keep.tile([P, CHUNKS * TAPS, P], U8, align_bytes=64)
        w_sorted, w_flipped, w_grouped, acc = {}, {}, {}, {}

        def sort(chunk, engine):
            by_tap = w_raw[chunk][:].rearrange("o (p u h t) -> o t p u h", u=WORDS, h=2, t=TAPS)
            if chunk not in w_sorted:
                words = stage.tile([P, TAPS * WORDS * P * 2], BF16, name="words")
                w_sorted[chunk] = words
            by_word = w_sorted[chunk][:].rearrange("o (t u p h) -> o t p u h", t=TAPS, u=WORDS, h=2)
            width = P // PIECES[chunk]
            for first in range(0, P, width):
                piece = slice(first, first + width)
                for group, taps in enumerate(GROUPS):
                    scalar_sorts = group == 1 and chunk < SCALAR_SORTS
                    if engine == "scalar" and scalar_sorts:
                        nc.scalar.copy(out=by_word[:, taps, piece], in_=by_tap[:, taps, piece])
                    if engine == "vector" and not scalar_sorts:
                        nc.vector.tensor_copy(out=by_word[:, taps, piece], in_=by_tap[:, taps, piece])

        def warm_up(count):
            for turn in range(count):
                scratch = acc_pool.tile([P, P], F32, name="acc")
                nc.tensor.matmul(scratch[:], lhsT=identity[:], rhs=identity[:], start=True, stop=True)

        def flip(chunk):
            words = w_sorted[chunk][:].bitcast(F32).rearrange("o (t u p) -> o t u p", t=TAPS, u=WORDS)
            for group, taps in enumerate(GROUPS):
                flipped = flipped_pool.tile(
                    [P, taps.stop - taps.start, WORDS, P], F32, name="flipped%d" % group, bufs=FLIPPED_BANKS[group]
                )
                for t in range(taps.start, taps.stop):
                    for u in range(WORDS):
                        nc.tensor.transpose(flipped[:, t - taps.start, u, :], words[:, t, u], identity[:])
                w_flipped[chunk, group] = flipped

        def gather(chunk, group):
            ot, g = divmod(chunk, PASSES)
            if ot not in w_grouped:
                grouped = stage.tile([P, PASSES * TAPS, P * PACK], BF16, name="grouped", align_bytes=64)
                w_grouped[ot] = grouped
            units = w_grouped[ot][:, g * TAPS + GROUPS[group].start : g * TAPS + GROUPS[group].stop]
            nc.scalar.copy(
                out=units.bitcast(F32).rearrange("p t (o u) -> p t o u", u=WORDS),
                in_=w_flipped[chunk, group][:].rearrange("p t u o -> p t o u"),
            )

        def quantise(ot, first, last):
            units = slice(ot * PASSES * TAPS + first, ot * PASSES * TAPS + last)
            nc.vector.quantize_mx(
                out=w_codes[:, units].rearrange("p i o -> p (i o)").bitcast(FP8X4),
                scales=w_scales[:, units].rearrange("p i o -> p (i o)"),
                in_=w_grouped[ot][:, first:last].rearrange("p i n -> p (i n)"),
            )

        def multiply(chunk):
            ot, g = divmod(chunk, PASSES)
            if g == 0:
                acc[ot] = acc_pool.tile([P, PIXELS], F32, name="acc")
            for t in range(TAPS):
                nc.tensor.matmul_mx(
                    out=acc[ot][:],
                    lhsT=w_codes[:, chunk * TAPS + t].bitcast(FP8X4),
                    lhsT_scale=w_scales[:, chunk * TAPS + t],
                    rhs=x_codes[:, t, g].rearrange("p b h w -> p (b h w)").bitcast(FP8X4),
                    rhs_scale=x_scales[:, t, g].rearrange("p b h w -> p (b h w)"),
                    start=(g == 0 and t == 0),
                    stop=(g == PASSES - 1 and t == TAPS - 1),
                )

        def store(ot):
            result = keep.tile([P, B, H * W], F32, name="result%d" % ot)
            nc.scalar.copy(out=result[:].rearrange("p b s -> p (b s)"), in_=acc[ot][:])
            nc.sync.dma_start(out=out[:, ot * P : (ot + 1) * P].rearrange("b o h w -> o b (h w)"), in_=result[:])

        warm_up(WARMING)
        group_x()
        sort(0, "vector")
        sort(0, "scalar")
        quantise_x()
        sort(1, "vector")
        sort(1, "scalar")
        shift_x(x_codes[:].bitcast(I32))
        shift_x(x_scales[:])
        for rnd in range(CHUNKS + MULTIPLY_LAG):
            if rnd + SORT_LEAD < CHUNKS:
                sort(rnd + SORT_LEAD, "vector")
            if rnd < CHUNKS:
                flip(rnd)
                if rnd in WARM_ROUNDS:
                    warm_up(1)
                for group in range(len(GROUPS)):
                    gather(rnd, group)
            if rnd + SORT_LEAD < CHUNKS:
                sort(rnd + SORT_LEAD, "scalar")
            for ot, first, last in QUANTISED.get(rnd, ()):
                quantise(ot, first, last)
            if 0 <= rnd - MULTIPLY_LAG < CHUNKS:
                multiply(rnd - MULTIPLY_LAG)
                if (rnd - MULTIPLY_LAG) % PASSES == PASSES - 1:
                    store((rnd - MULTIPLY_LAG) // PASSES)
